import numpy as np
import ml_dtypes


def mxq(x, axis, fmt="e4m3"):
    dtype, down = {"e4m3": (ml_dtypes.float8_e4m3fn, 7), "e5m2": (ml_dtypes.float8_e5m2, 14)}[fmt]
    v = np.moveaxis(np.asarray(x, np.float32).astype(ml_dtypes.bfloat16).astype(np.float64), axis, -1)
    blocks = v.reshape(v.shape[:-1] + (-1, 32))
    amax = np.abs(blocks).max(-1, keepdims=True)
    byte = np.maximum(np.where(amax > 0, np.frexp(amax)[1] - 1 + 127, 0) - down, 1)
    scale = np.exp2(byte - 127.0)
    codes = (blocks / scale).astype(np.float32).astype(dtype).astype(np.float64)
    return np.moveaxis((codes * scale).reshape(v.shape), -1, axis)


WIDE = False


def mx_kscale(k):
    if not WIDE:
        return np.ones(k)
    levels = np.array([10, -10, 5, -5, 0])
    a = np.random.permutation(np.resize(levels, k // 512 * 4)).reshape(k // 512, 4)
    idx = np.arange(k)
    return np.exp2(a[idx // 512, idx % 128 // 32])


BF16 = ml_dtypes.bfloat16


def bf(x):
    return np.asarray(x, np.float32).astype(BF16)


def f64(x):
    return np.asarray(x).astype(np.float64)


E2M1 = np.array([0.0, 0.5, 1.0, 1.5, 2.0, 3.0, 4.0, 6.0, -0.0, -0.5, -1.0, -1.5, -2.0, -3.0, -4.0, -6.0])


def pack_weight(w, fmt):
    k, n = w.shape
    w = f64(bf(w)).reshape(k // 32, 32, n)
    amax = np.abs(w).max(1)
    if fmt == "e4m3":
        byte = np.frexp(amax)[1] - 1 + 127 - 7
    else:
        mant, ex = np.frexp(amax / 6.0)
        byte = np.where(mant > 0.5, ex, ex - 1) + 127
    byte = np.clip(np.where(amax > 0, byte, 1), 1, 254)
    scaled = (w * np.exp2(127.0 - byte)[:, None, :]).reshape(k, n).astype(np.float32)
    by_word = np.ascontiguousarray(scaled.reshape(k // 512, 128, 4, n).transpose(0, 1, 3, 2))
    if fmt == "e4m3":
        words = by_word.astype(ml_dtypes.float8_e4m3fn).view(np.uint8)
    else:
        c = by_word.astype(ml_dtypes.float4_e2m1fn).view(np.uint8) & 0xF
        words = c[..., 0::2] | (c[..., 1::2] << 4)
    return np.ascontiguousarray(words), np.ascontiguousarray(byte.astype(np.uint8).reshape(k // 512, 16, n))


def unpack_weight(words, scales, fmt):
    g, p, n, _ = words.shape
    if fmt == "e4m3":
        vals = np.ascontiguousarray(words).view(ml_dtypes.float8_e4m3fn).astype(np.float64)
    else:
        nib = np.empty((g, p, n, 4), np.uint8)
        nib[..., 0::2] = words & 0xF
        nib[..., 1::2] = words >> 4
        vals = E2M1[nib]
    vals = vals * np.repeat(np.exp2(scales.astype(np.float64) - 127.0), 8, axis=1)[..., None]
    return vals.transpose(0, 1, 3, 2).reshape(g * 512, n)

def pack4(w):
    words, scales = pack_weight(w, "e2m1")
    return words.reshape(words.shape[0], 128, -1), scales


def unpack4(words, scales):
    return unpack_weight(words.reshape(words.shape[0], 128, -1, 2), scales, "e2m1")


B, T, C, H, NOPE, ROPE, VD, LORA = 1, 512, 2048, 16, 128, 128, 128, 512
QK = NOPE + ROPE
HALF = ROPE // 2


def make_freq_cis():
    inv = 1.0 / (10000.0 ** (np.arange(0, ROPE, 2) / ROPE))
    ang = np.outer(np.arange(T), inv)
    return np.stack([np.cos(ang), np.sin(ang)], -1)


def apply_rope(v, fc):
    vr = v.reshape(B, T, H, HALF, 2)
    f = fc.reshape(1, T, 1, HALF, 2)
    real = vr[..., 0] * f[..., 0] - vr[..., 1] * f[..., 1]
    imag = vr[..., 1] * f[..., 0] + vr[..., 0] * f[..., 1]
    return np.stack([real, imag], -1).reshape(B, T, H, ROPE)


def setup_inputs():
    s = mx_kscale(C)
    x = bf(np.random.standard_normal((B, T, C)) * s)
    freq_cis = bf(make_freq_cis())
    words, scales = pack4(np.random.standard_normal((C, H * QK)) * 2.0 / np.sqrt(C) / s[:, None])
    return {"x": x,
            "freq_cis": freq_cis,
            "Wq_words": words,
            "Wq_scales": scales}


def reference(x, freq_cis, Wq_words, Wq_scales):
    q = (mxq(f64(x), 2, "e4m3") @ unpack4(Wq_words, Wq_scales)).reshape(B, T, H, QK)
    q_nope, q_rope = q[..., :NOPE], q[..., NOPE:]
    q_rope = apply_rope(q_rope, f64(freq_cis))
    return np.concatenate([q_nope, q_rope], -1)

@@ -1,0 +1,174 @@
+import concourse.bass as bass
+import concourse.mybir as mybir
+import concourse.tile as tile
+from concourse.masks import make_identity
+
+F32 = mybir.dt.float32
+BF16 = mybir.dt.bfloat16
+I32 = mybir.dt.int32
+U32 = mybir.dt.uint32
+U8 = mybir.dt.uint8
+FP8X4 = mybir.dt.float8_e4m3fn_x4
+FP4X4 = mybir.dt.float4_e2m1fn_x4
+MULT = mybir.AluOpType.mult
+ADD = mybir.AluOpType.add
+
+P = 128
+PACK = 4
+K_PASS = P * PACK
+
+TOKENS = 512
+K = 2048
+HEADS = 16
+NOPE = 128
+ROPE = 128
+QK = NOPE + ROPE
+PAIRS = ROPE // 2
+N = HEADS * QK
+
+TOKEN_TILES = TOKENS // P
+GROUPS = K // K_PASS
+N_TILE = 512
+BANK_HEADS = N_TILE // QK
+CHUNKS = N // N_TILE
+WORDS_PER_GROUP = K_PASS // 2
+
+SCALE_CHUNKS = 2
+SCALE_COLS = SCALE_CHUNKS * N_TILE
+
+FLOPS = 2 * TOKENS * K * N
+
+
+def tile_multiheadlatentattention_pb_kernel(tc, x, freq_cis, Wq_words, Wq_scales, out):
+    nc = tc.nc
+    x_rows_dram = x.rearrange("b t k -> (b t) k")
+    out_rows_dram = out.rearrange("b t h d -> (b t) (h d)")
+    words_dram = Wq_words.rearrange("g p b -> p g b")
+    scales_dram = Wq_scales.rearrange("g q n -> q g n")
+
+    with tc.tile_pool(name="keep", bufs=1) as keep, tc.tile_pool(
+        name="x_in", bufs=TOKEN_TILES
+    ) as x_in, tc.tile_pool(name="w_in", bufs=CHUNKS) as w_in, tc.tile_pool(
+        name="s_in", bufs=CHUNKS // SCALE_CHUNKS
+    ) as s_in, tc.tile_pool(name="results", bufs=8) as results:
+        w_planes = []
+        for c in range(CHUNKS // SCALE_CHUNKS):
+            plane = s_in.tile([P, GROUPS, SCALE_COLS], U8, align_bytes=64)
+            nc.vector.memset(plane[:].bitcast(I32), 0)
+            w_planes.append(plane)
+
+        table = keep.tile([P, TOKEN_TILES, PAIRS, 2], BF16)
+        nc.scalar.dma_start(out=table[:], in_=freq_cis.rearrange("(m p) i e -> p m i e", p=P))
+
+        x_tiles = []
+        for m in range(TOKEN_TILES):
+            x_rows = x_in.tile([P, K], BF16)
+            nc.sync.dma_start(out=x_rows[:], in_=x_rows_dram[m * P : (m + 1) * P, :])
+            x_tiles.append(x_rows)
+
+        w_chunks = []
+        for c in range(CHUNKS // SCALE_CHUNKS):
+            cols = slice(c * SCALE_COLS, (c + 1) * SCALE_COLS)
+            for b in range(2):
+                for r in range(4):
+                    nc.sync.dma_start(
+                        out=w_planes[c][32 * b + r : P : 64, :, :].bitcast(I32),
+                        in_=scales_dram[4 * b + r : 16 : 8, :, cols].bitcast(I32),
+                    )
+            for j in range(c * SCALE_CHUNKS, (c + 1) * SCALE_CHUNKS):
+                w_chunk = w_in.tile([P, GROUPS, 2 * N_TILE], U8, align_bytes=64)
+                nc.sync.dma_start(
+                    out=w_chunk[:].bitcast(I32),
+                    in_=words_dram[:, :, j * 2 * N_TILE : (j + 1) * 2 * N_TILE].bitcast(I32),
+                )
+                w_chunks.append(w_chunk)
+
+        cos_pair = keep.tile([P, TOKEN_TILES, PAIRS, 2], F32)
+        sin_signed = keep.tile([P, TOKEN_TILES, 2, PAIRS], F32)
+        nc.vector.tensor_copy(
+            out=cos_pair[:], in_=table[:, :, :, 0:1].to_broadcast([P, TOKEN_TILES, PAIRS, 2])
+        )
+        nc.vector.tensor_scalar_mul(out=sin_signed[:, :, 0, :], in0=table[:, :, :, 1], scalar1=-1.0)
+        nc.vector.tensor_copy(out=sin_signed[:, :, 1, :], in_=table[:, :, :, 1])
+
+        identity = keep.tile([P, P], F32)
+        make_identity(nc, identity[:])
+        x_codes = keep.tile([P, TOKEN_TILES, GROUPS, P], U32, align_bytes=64)
+        x_scales = keep.tile([P, TOKEN_TILES, GROUPS, P], U8, align_bytes=64)
+
+        with tc.psum_pool(name="turned", bufs=8) as turned_pool:
+            for m in range(TOKEN_TILES):
+                x_words = x_tiles[m][:].bitcast(F32)
+                grouped = x_in.tile([P, GROUPS, P, PACK], BF16, align_bytes=64)
+                grouped_words = grouped[:].bitcast(F32)
+                for half in range(2):
+                    turned = turned_pool.tile([P, 2, 2, P], F32)
+                    for gg in range(2):
+                        g = 2 * half + gg
+                        for u in range(2):
+                            nc.tensor.transpose(
+                                out=turned[:, gg, u, :],
+                                in_=x_words[:, g * WORDS_PER_GROUP + u : (g + 1) * WORDS_PER_GROUP : 2],
+                                identity=identity[:],
+                            )
+                    source = turned[:].rearrange("p g u r -> p g r u")
+                    target = grouped_words[:, 2 * half : 2 * half + 2, :, :]
+                    if half == 0:
+                        nc.vector.tensor_copy(out=target, in_=source)
+                    else:
+                        nc.scalar.copy(out=target, in_=source)
+                nc.vector.quantize_mx(
+                    out=x_codes[:, m, :, :].rearrange("p g r -> p (g r)").bitcast(FP8X4),
+                    scales=x_scales[:, m, :, :].rearrange("p g r -> p (g r)"),
+                    in_=grouped[:].rearrange("p g r t -> p (g r t)"),
+                )
+
+        with tc.psum_pool(name="sums", bufs=8, reuse_waits="tile") as sums_pool, tc.tile_pool(
+            name="crossed", bufs=4
+        ) as crossed_pool:
+            for j in range(CHUNKS):
+                plane = w_planes[j // SCALE_CHUNKS]
+                plane_cols = slice((j % SCALE_CHUNKS) * N_TILE, (j % SCALE_CHUNKS + 1) * N_TILE)
+                for m in range(TOKEN_TILES):
+                    sums = sums_pool.tile([P, BANK_HEADS, QK], F32)
+                    for g in range(GROUPS):
+                        nc.tensor.matmul_mx(
+                            out=sums[:].rearrange("p h d -> p (h d)"),
+                            lhsT=x_codes[:, m, g, :].bitcast(FP8X4),
+                            lhsT_scale=x_scales[:, m, g, :],
+                            rhs=w_chunks[j][:, g, :].bitcast(FP4X4),
+                            rhs_scale=plane[:, g, plane_cols],
+                            start=(g == 0),
+                            stop=(g == GROUPS - 1),
+                        )
+                    result = results.tile([P, BANK_HEADS, QK], F32)
+                    crossed = crossed_pool.tile([P, BANK_HEADS, 2, PAIRS], F32)
+                    pairs = sums[:, :, NOPE:].rearrange("p h (i e) -> p h i e", e=2)
+                    nc.vector.tensor_tensor(
+                        out=result[:, :, NOPE:],
+                        in0=sums[:, :, NOPE:],
+                        in1=cos_pair[:, m, :, :]
+                        .rearrange("p i e -> p (i e)")
+                        .unsqueeze(1)
+                        .to_broadcast([P, BANK_HEADS, ROPE]),
+                        op=MULT,
+                    )
+                    for e in range(2):
+                        nc.vector.tensor_tensor(
+                            out=crossed[:, :, e, :],
+                            in0=pairs[:, :, :, 1 - e],
+                            in1=sin_signed[:, m, e, :].unsqueeze(1).to_broadcast([P, BANK_HEADS, PAIRS]),
+                            op=MULT,
+                        )
+                    nc.scalar.copy(out=result[:, :, :NOPE], in_=sums[:, :, :NOPE])
+                    rotated = result[:, :, NOPE:].rearrange("p h (i e) -> p h i e", e=2)
+                    nc.vector.tensor_tensor(
+                        out=rotated,
+                        in0=rotated,
+                        in1=crossed[:].rearrange("p h e i -> p h i e"),
+                        op=ADD,
+                    )
+                    nc.sync.dma_start(
+                        out=out_rows_dram[m * P : (m + 1) * P, j * N_TILE : (j + 1) * N_TILE],
+                        in_=result[:].rearrange("p h d -> p (h d)"),
+                    )

@@ -60,21 +60,26 @@ def tile_multiheadlatentattention_pb_kernel(tc, x, freq_cis, Wq_words, Wq_scales
         table = keep.tile([P, TOKEN_TILES, PAIRS, 2], BF16)
         nc.scalar.dma_start(out=table[:], in_=freq_cis.rearrange("(m p) i e -> p m i e", p=P))
 
+        def load_scales(c):
+            cols = slice(c * SCALE_COLS, (c + 1) * SCALE_COLS)
+            for r in range(4):
+                nc.sync.dma_start(
+                    out=w_planes[c][r : P : 32, :, :].bitcast(I32),
+                    in_=scales_dram[r : 16 : 4, :, cols].bitcast(I32),
+                )
+
         x_tiles = []
         for m in range(TOKEN_TILES):
             x_rows = x_in.tile([P, K], BF16)
             nc.sync.dma_start(out=x_rows[:], in_=x_rows_dram[m * P : (m + 1) * P, :])
             x_tiles.append(x_rows)
+            if m == 0:
+                load_scales(0)
 
         w_chunks = []
         for c in range(CHUNKS // SCALE_CHUNKS):
-            cols = slice(c * SCALE_COLS, (c + 1) * SCALE_COLS)
-            for b in range(2):
-                for r in range(4):
-                    nc.sync.dma_start(
-                        out=w_planes[c][32 * b + r : P : 64, :, :].bitcast(I32),
-                        in_=scales_dram[4 * b + r : 16 : 8, :, cols].bitcast(I32),
-                    )
+            if c > 0:
+                load_scales(c)
             for j in range(c * SCALE_CHUNKS, (c + 1) * SCALE_CHUNKS):
                 w_chunk = w_in.tile([P, GROUPS, 2 * N_TILE], U8, align_bytes=64)
                 nc.sync.dma_start(

@@ -167,7 +167,7 @@ def tile_multiheadlatentattention_pb_kernel(tc, x, freq_cis, Wq_words, Wq_scales
                         )
                     nc.scalar.copy(out=result[:, :, :NOPE], in_=sums[:, :, :NOPE])
                     rotated = result[:, :, NOPE:].rearrange("p h (i e) -> p h i e", e=2)
-                    nc.vector.tensor_tensor(
+                    nc.gpsimd.tensor_tensor(
                         out=rotated,
                         in0=rotated,
                         in1=crossed[:].rearrange("p h e i -> p h i e"),

@@ -36,6 +36,9 @@ WORDS_PER_GROUP = K_PASS // 2
 SCALE_CHUNKS = 2
 SCALE_COLS = SCALE_CHUNKS * N_TILE
 
+WARM_FIRST = 6
+WARM_BETWEEN = 2
+
 FLOPS = 2 * TOKENS * K * N
 
 
@@ -51,6 +54,8 @@ def tile_multiheadlatentattention_pb_kernel(tc, x, freq_cis, Wq_words, Wq_scales
     ) as x_in, tc.tile_pool(name="w_in", bufs=CHUNKS) as w_in, tc.tile_pool(
         name="s_in", bufs=CHUNKS // SCALE_CHUNKS
     ) as s_in, tc.tile_pool(name="results", bufs=8) as results:
+        zeros = keep.tile([P, N_TILE], BF16)
+        nc.vector.memset(zeros[:], 0.0)
         w_planes = []
         for c in range(CHUNKS // SCALE_CHUNKS):
             plane = s_in.tile([P, GROUPS, SCALE_COLS], U8, align_bytes=64)
@@ -101,7 +106,16 @@ def tile_multiheadlatentattention_pb_kernel(tc, x, freq_cis, Wq_words, Wq_scales
         x_codes = keep.tile([P, TOKEN_TILES, GROUPS, P], U32, align_bytes=64)
         x_scales = keep.tile([P, TOKEN_TILES, GROUPS, P], U8, align_bytes=64)
 
-        with tc.psum_pool(name="turned", bufs=8) as turned_pool:
+        with tc.psum_pool(name="turned", bufs=7) as turned_pool, tc.psum_pool(
+            name="warm", bufs=1
+        ) as warm_pool, tc.manual_schedule(engines={mybir.EngineType.PE}):
+            warm = warm_pool.tile([P, N_TILE], F32)
+
+            def dummies(count):
+                for i in range(count):
+                    nc.tensor.matmul(out=warm[:], lhsT=zeros[:, :P], rhs=zeros[:], start=True, stop=True)
+
+            dummies(WARM_FIRST)
             for m in range(TOKEN_TILES):
                 x_words = x_tiles[m][:].bitcast(F32)
                 grouped = x_in.tile([P, GROUPS, P, PACK], BF16, align_bytes=64)
@@ -127,6 +141,7 @@ def tile_multiheadlatentattention_pb_kernel(tc, x, freq_cis, Wq_words, Wq_scales
                     scales=x_scales[:, m, :, :].rearrange("p g r -> p (g r)"),
                     in_=grouped[:].rearrange("p g r t -> p (g r t)"),
                 )
+                dummies(WARM_BETWEEN)
 
         with tc.psum_pool(name="sums", bufs=8, reuse_waits="tile") as sums_pool, tc.tile_pool(
             name="crossed", bufs=4

@@ -36,8 +36,7 @@ WORDS_PER_GROUP = K_PASS // 2
 SCALE_CHUNKS = 2
 SCALE_COLS = SCALE_CHUNKS * N_TILE
 
-WARM_FIRST = 6
-WARM_BETWEEN = 2
+WARM_FIRST = 4
 
 FLOPS = 2 * TOKENS * K * N
 
@@ -46,6 +45,7 @@ def tile_multiheadlatentattention_pb_kernel(tc, x, freq_cis, Wq_words, Wq_scales
     nc = tc.nc
     x_rows_dram = x.rearrange("b t k -> (b t) k")
     out_rows_dram = out.rearrange("b t h d -> (b t) (h d)")
+    out_heads_dram = out.rearrange("b t h d -> (b t) h d")
     words_dram = Wq_words.rearrange("g p b -> p g b")
     scales_dram = Wq_scales.rearrange("g q n -> q g n")
 
@@ -53,7 +53,11 @@ def tile_multiheadlatentattention_pb_kernel(tc, x, freq_cis, Wq_words, Wq_scales
         name="x_in", bufs=TOKEN_TILES
     ) as x_in, tc.tile_pool(name="w_in", bufs=CHUNKS) as w_in, tc.tile_pool(
         name="s_in", bufs=CHUNKS // SCALE_CHUNKS
-    ) as s_in, tc.tile_pool(name="results", bufs=8) as results:
+    ) as s_in, tc.tile_pool(name="results", bufs=8) as results, tc.tile_pool(
+        name="crossed", bufs=4
+    ) as crossed_pool, tc.psum_pool(name="turned", bufs=4) as turned_pool, tc.psum_pool(
+        name="sums", bufs=4, reuse_waits="tile"
+    ) as sums_pool, tc.manual_schedule(engines={mybir.EngineType.PE}):
         zeros = keep.tile([P, N_TILE], BF16)
         nc.vector.memset(zeros[:], 0.0)
         w_planes = []
@@ -74,24 +78,35 @@ def tile_multiheadlatentattention_pb_kernel(tc, x, freq_cis, Wq_words, Wq_scales
                 )
 
         x_tiles = []
-        for m in range(TOKEN_TILES):
+
+        def load_x(m):
             x_rows = x_in.tile([P, K], BF16)
             nc.sync.dma_start(out=x_rows[:], in_=x_rows_dram[m * P : (m + 1) * P, :])
             x_tiles.append(x_rows)
-            if m == 0:
-                load_scales(0)
 
         w_chunks = []
-        for c in range(CHUNKS // SCALE_CHUNKS):
-            if c > 0:
-                load_scales(c)
-            for j in range(c * SCALE_CHUNKS, (c + 1) * SCALE_CHUNKS):
-                w_chunk = w_in.tile([P, GROUPS, 2 * N_TILE], U8, align_bytes=64)
+
+        def load_words(j, pieces):
+            w_chunk = w_in.tile([P, GROUPS, 2 * N_TILE], U8, align_bytes=64)
+            step = GROUPS // pieces
+            for g0 in range(0, GROUPS, step):
                 nc.sync.dma_start(
-                    out=w_chunk[:].bitcast(I32),
-                    in_=words_dram[:, :, j * 2 * N_TILE : (j + 1) * 2 * N_TILE].bitcast(I32),
+                    out=w_chunk[:, g0 : g0 + step, :].bitcast(I32),
+                    in_=words_dram[:, g0 : g0 + step, j * 2 * N_TILE : (j + 1) * 2 * N_TILE].bitcast(I32),
                 )
-                w_chunks.append(w_chunk)
+            w_chunks.append(w_chunk)
+
+        load_x(0)
+        load_x(1)
+        load_scales(0)
+        load_words(0, 2)
+        load_x(2)
+        load_x(3)
+        load_words(1, 1)
+        for c in range(1, CHUNKS // SCALE_CHUNKS):
+            load_scales(c)
+            for j in range(c * SCALE_CHUNKS, (c + 1) * SCALE_CHUNKS):
+                load_words(j, 1)
 
         cos_pair = keep.tile([P, TOKEN_TILES, PAIRS, 2], F32)
         sin_signed = keep.tile([P, TOKEN_TILES, 2, PAIRS], F32)
@@ -106,89 +121,111 @@ def tile_multiheadlatentattention_pb_kernel(tc, x, freq_cis, Wq_words, Wq_scales
         x_codes = keep.tile([P, TOKEN_TILES, GROUPS, P], U32, align_bytes=64)
         x_scales = keep.tile([P, TOKEN_TILES, GROUPS, P], U8, align_bytes=64)
 
-        with tc.psum_pool(name="turned", bufs=7) as turned_pool, tc.psum_pool(
-            name="warm", bufs=1
-        ) as warm_pool, tc.manual_schedule(engines={mybir.EngineType.PE}):
-            warm = warm_pool.tile([P, N_TILE], F32)
+        turned = turned_pool.tile([P, 2, 2, P], F32)
+        for i in range(WARM_FIRST):
+            nc.tensor.matmul(
+                out=turned[:].rearrange("p g u r -> p (g u r)"), lhsT=zeros[:, :P], rhs=zeros[:], start=True, stop=True
+            )
 
-            def dummies(count):
-                for i in range(count):
-                    nc.tensor.matmul(out=warm[:], lhsT=zeros[:, :P], rhs=zeros[:], start=True, stop=True)
-
-            dummies(WARM_FIRST)
-            for m in range(TOKEN_TILES):
-                x_words = x_tiles[m][:].bitcast(F32)
-                grouped = x_in.tile([P, GROUPS, P, PACK], BF16, align_bytes=64)
-                grouped_words = grouped[:].bitcast(F32)
-                for half in range(2):
-                    turned = turned_pool.tile([P, 2, 2, P], F32)
-                    for gg in range(2):
-                        g = 2 * half + gg
-                        for u in range(2):
-                            nc.tensor.transpose(
-                                out=turned[:, gg, u, :],
-                                in_=x_words[:, g * WORDS_PER_GROUP + u : (g + 1) * WORDS_PER_GROUP : 2],
-                                identity=identity[:],
-                            )
-                    source = turned[:].rearrange("p g u r -> p g r u")
-                    target = grouped_words[:, 2 * half : 2 * half + 2, :, :]
-                    if half == 0:
-                        nc.vector.tensor_copy(out=target, in_=source)
-                    else:
-                        nc.scalar.copy(out=target, in_=source)
-                nc.vector.quantize_mx(
-                    out=x_codes[:, m, :, :].rearrange("p g r -> p (g r)").bitcast(FP8X4),
-                    scales=x_scales[:, m, :, :].rearrange("p g r -> p (g r)"),
-                    in_=grouped[:].rearrange("p g r t -> p (g r t)"),
+        def turn(m):
+            x_words = x_tiles[m][:].bitcast(F32)
+            grouped = x_in.tile([P, GROUPS, P, PACK], BF16, align_bytes=64)
+            grouped_words = grouped[:].bitcast(F32)
+            for half in range(2):
+                turned = turned_pool.tile([P, 2, 2, P], F32)
+                for gg in range(2):
+                    g = 2 * half + gg
+                    for u in range(2):
+                        nc.tensor.transpose(
+                            out=turned[:, gg, u, :],
+                            in_=x_words[:, g * WORDS_PER_GROUP + u : (g + 1) * WORDS_PER_GROUP : 2],
+                            identity=identity[:],
+                        )
+                nc.scalar.copy(
+                    out=grouped_words[:, 2 * half : 2 * half + 2, :, :],
+                    in_=turned[:].rearrange("p g u r -> p g r u"),
                 )
-                dummies(WARM_BETWEEN)
+                nc.vector.quantize_mx(
+                    out=x_codes[:, m, 2 * half : 2 * half + 2, :].rearrange("p g r -> p (g r)").bitcast(FP8X4),
+                    scales=x_scales[:, m, 2 * half : 2 * half + 2, :].rearrange("p g r -> p (g r)"),
+                    in_=grouped[:, 2 * half : 2 * half + 2, :, :].rearrange("p g r t -> p (g r t)"),
+                )
 
-        with tc.psum_pool(name="sums", bufs=8, reuse_waits="tile") as sums_pool, tc.tile_pool(
-            name="crossed", bufs=4
-        ) as crossed_pool:
-            for j in range(CHUNKS):
-                plane = w_planes[j // SCALE_CHUNKS]
-                plane_cols = slice((j % SCALE_CHUNKS) * N_TILE, (j % SCALE_CHUNKS + 1) * N_TILE)
-                for m in range(TOKEN_TILES):
-                    sums = sums_pool.tile([P, BANK_HEADS, QK], F32)
-                    for g in range(GROUPS):
-                        nc.tensor.matmul_mx(
-                            out=sums[:].rearrange("p h d -> p (h d)"),
-                            lhsT=x_codes[:, m, g, :].bitcast(FP8X4),
-                            lhsT_scale=x_scales[:, m, g, :],
-                            rhs=w_chunks[j][:, g, :].bitcast(FP4X4),
-                            rhs_scale=plane[:, g, plane_cols],
-                            start=(g == 0),
-                            stop=(g == GROUPS - 1),
-                        )
-                    result = results.tile([P, BANK_HEADS, QK], F32)
-                    crossed = crossed_pool.tile([P, BANK_HEADS, 2, PAIRS], F32)
-                    pairs = sums[:, :, NOPE:].rearrange("p h (i e) -> p h i e", e=2)
-                    nc.vector.tensor_tensor(
-                        out=result[:, :, NOPE:],
-                        in0=sums[:, :, NOPE:],
-                        in1=cos_pair[:, m, :, :]
-                        .rearrange("p i e -> p (i e)")
-                        .unsqueeze(1)
-                        .to_broadcast([P, BANK_HEADS, ROPE]),
-                        op=MULT,
-                    )
-                    for e in range(2):
-                        nc.vector.tensor_tensor(
-                            out=crossed[:, :, e, :],
-                            in0=pairs[:, :, :, 1 - e],
-                            in1=sin_signed[:, m, e, :].unsqueeze(1).to_broadcast([P, BANK_HEADS, PAIRS]),
-                            op=MULT,
-                        )
-                    nc.scalar.copy(out=result[:, :, :NOPE], in_=sums[:, :, :NOPE])
-                    rotated = result[:, :, NOPE:].rearrange("p h (i e) -> p h i e", e=2)
-                    nc.gpsimd.tensor_tensor(
-                        out=rotated,
-                        in0=rotated,
-                        in1=crossed[:].rearrange("p h e i -> p h i e"),
-                        op=ADD,
-                    )
-                    nc.sync.dma_start(
-                        out=out_rows_dram[m * P : (m + 1) * P, j * N_TILE : (j + 1) * N_TILE],
-                        in_=result[:].rearrange("p h d -> p (h d)"),
-                    )
+        def passes(target, j, m, first_col, width):
+            plane = w_planes[j // SCALE_CHUNKS]
+            plane_col = (j % SCALE_CHUNKS) * N_TILE + first_col
+            for g in range(GROUPS):
+                nc.tensor.matmul_mx(
+                    out=target,
+                    lhsT=x_codes[:, m, g, :].bitcast(FP8X4),
+                    lhsT_scale=x_scales[:, m, g, :],
+                    rhs=w_chunks[j][:, g, 2 * first_col : 2 * (first_col + width)].bitcast(FP4X4),
+                    rhs_scale=plane[:, g, plane_col : plane_col + width],
+                    start=(g == 0),
+                    stop=(g == GROUPS - 1),
+                )
+
+        def rotate(rope_sums, rope_result, m, adder):
+            crossed = crossed_pool.tile([P, BANK_HEADS, 2, PAIRS], F32)
+            pairs = rope_sums.rearrange("p h (i e) -> p h i e", e=2)
+            nc.vector.tensor_tensor(
+                out=rope_result,
+                in0=rope_sums,
+                in1=cos_pair[:, m, :, :]
+                .rearrange("p i e -> p (i e)")
+                .unsqueeze(1)
+                .to_broadcast([P, BANK_HEADS, ROPE]),
+                op=MULT,
+            )
+            for e in range(2):
+                nc.vector.tensor_tensor(
+                    out=crossed[:, :, e, :],
+                    in0=pairs[:, :, :, 1 - e],
+                    in1=sin_signed[:, m, e, :].unsqueeze(1).to_broadcast([P, BANK_HEADS, PAIRS]),
+                    op=MULT,
+                )
+            rotated = rope_result.rearrange("p h (i e) -> p h i e", e=2)
+            adder.tensor_tensor(
+                out=rotated, in0=rotated, in1=crossed[:].rearrange("p h e i -> p h i e"), op=ADD
+            )
+
+        def multiply(j, m):
+            sums = sums_pool.tile([P, BANK_HEADS, QK], F32)
+            passes(sums[:].rearrange("p h d -> p (h d)"), j, m, 0, N_TILE)
+            result = results.tile([P, BANK_HEADS, QK], F32)
+            rotate(sums[:, :, NOPE:], result[:, :, NOPE:], m, nc.gpsimd)
+            nc.scalar.copy(out=result[:, :, :NOPE], in_=sums[:, :, :NOPE])
+            nc.sync.dma_start(
+                out=out_rows_dram[m * P : (m + 1) * P, j * N_TILE : (j + 1) * N_TILE],
+                in_=result[:].rearrange("p h d -> p (h d)"),
+            )
+
+        def multiply_last(j, m):
+            result = results.tile([P, BANK_HEADS, QK], F32)
+            rows = slice(m * P, (m + 1) * P)
+            heads = slice(j * BANK_HEADS, (j + 1) * BANK_HEADS)
+            sums = sums_pool.tile([P, BANK_HEADS, ROPE], F32)
+            for h in range(BANK_HEADS):
+                passes(sums[:, h, :], j, m, h * QK + NOPE, ROPE)
+            rotate(sums[:], result[:, :, NOPE:], m, nc.vector)
+            nc.sync.dma_start(out=out_heads_dram[rows, heads, NOPE:], in_=result[:, :, NOPE:])
+            sums = sums_pool.tile([P, BANK_HEADS, NOPE], F32)
+            for h in range(BANK_HEADS):
+                passes(sums[:, h, :], j, m, h * QK, NOPE)
+            nc.scalar.copy(out=result[:, :, :NOPE], in_=sums[:])
+            nc.sync.dma_start(out=out_heads_dram[rows, heads, :NOPE], in_=result[:, :, :NOPE])
+
+        turn(0)
+        turn(1)
+        multiply(0, 0)
+        multiply(0, 1)
+        turn(2)
+        turn(3)
+        multiply(0, 2)
+        multiply(0, 3)
+        for j in range(1, CHUNKS):
+            for m in range(TOKEN_TILES):
+                if (j, m) == (CHUNKS - 1, TOKEN_TILES - 1):
+                    multiply_last(j, m)
+                else:
+                    multiply(j, m)

@@ -53,8 +53,8 @@ def tile_multiheadlatentattention_pb_kernel(tc, x, freq_cis, Wq_words, Wq_scales
         name="x_in", bufs=TOKEN_TILES
     ) as x_in, tc.tile_pool(name="w_in", bufs=CHUNKS) as w_in, tc.tile_pool(
         name="s_in", bufs=CHUNKS // SCALE_CHUNKS
-    ) as s_in, tc.tile_pool(name="results", bufs=8) as results, tc.tile_pool(
-        name="crossed", bufs=4
+    ) as s_in, tc.tile_pool(name="results", bufs=32) as results, tc.tile_pool(
+        name="crossed", bufs=8
     ) as crossed_pool, tc.psum_pool(name="turned", bufs=4) as turned_pool, tc.psum_pool(
         name="sums", bufs=4, reuse_waits="tile"
     ) as sums_pool, tc.manual_schedule(engines={mybir.EngineType.PE}):

@@ -38,6 +38,8 @@ SCALE_COLS = SCALE_CHUNKS * N_TILE
 
 WARM_FIRST = 4
 
+PLANE_RUNS = ((0, 1), (1, 1), (2, 2), (4, 2), (6, 2))
+
 FLOPS = 2 * TOKENS * K * N
 
 
@@ -52,29 +54,31 @@ def tile_multiheadlatentattention_pb_kernel(tc, x, freq_cis, Wq_words, Wq_scales
     with tc.tile_pool(name="keep", bufs=1) as keep, tc.tile_pool(
         name="x_in", bufs=TOKEN_TILES
     ) as x_in, tc.tile_pool(name="w_in", bufs=CHUNKS) as w_in, tc.tile_pool(
-        name="s_in", bufs=CHUNKS // SCALE_CHUNKS
+        name="s_in", bufs=len(PLANE_RUNS)
     ) as s_in, tc.tile_pool(name="results", bufs=32) as results, tc.tile_pool(
         name="crossed", bufs=8
-    ) as crossed_pool, tc.psum_pool(name="turned", bufs=4) as turned_pool, tc.psum_pool(
+    ) as crossed_pool, tc.psum_pool(
         name="sums", bufs=4, reuse_waits="tile"
     ) as sums_pool, tc.manual_schedule(engines={mybir.EngineType.PE}):
         zeros = keep.tile([P, N_TILE], BF16)
         nc.vector.memset(zeros[:], 0.0)
-        w_planes = []
-        for c in range(CHUNKS // SCALE_CHUNKS):
-            plane = s_in.tile([P, GROUPS, SCALE_COLS], U8, align_bytes=64)
+        w_planes = {}
+        for first, count in PLANE_RUNS:
+            plane = s_in.tile([P, GROUPS, count * N_TILE], U8, align_bytes=64)
             nc.vector.memset(plane[:].bitcast(I32), 0)
-            w_planes.append(plane)
+            for j in range(first, first + count):
+                w_planes[j] = (plane, (j - first) * N_TILE)
 
         table = keep.tile([P, TOKEN_TILES, PAIRS, 2], BF16)
         nc.scalar.dma_start(out=table[:], in_=freq_cis.rearrange("(m p) i e -> p m i e", p=P))
+        primed = keep.tile([P, 1], BF16)
+        nc.scalar.copy(out=primed[:], in_=zeros[:, 0:1])
 
-        def load_scales(c):
-            cols = slice(c * SCALE_COLS, (c + 1) * SCALE_COLS)
+        def load_scales(j, count):
             for r in range(4):
                 nc.sync.dma_start(
-                    out=w_planes[c][r : P : 32, :, :].bitcast(I32),
-                    in_=scales_dram[r : 16 : 4, :, cols].bitcast(I32),
+                    out=w_planes[j][0][r : P : 32, :, :].bitcast(I32),
+                    in_=scales_dram[r : 16 : 4, :, j * N_TILE : (j + count) * N_TILE].bitcast(I32),
                 )
 
         x_tiles = []
@@ -97,14 +101,15 @@ def tile_multiheadlatentattention_pb_kernel(tc, x, freq_cis, Wq_words, Wq_scales
             w_chunks.append(w_chunk)
 
         load_x(0)
+        load_scales(0, 1)
         load_x(1)
-        load_scales(0)
         load_words(0, 2)
         load_x(2)
         load_x(3)
+        load_scales(1, 1)
         load_words(1, 1)
         for c in range(1, CHUNKS // SCALE_CHUNKS):
-            load_scales(c)
+            load_scales(c * SCALE_CHUNKS, SCALE_CHUNKS)
             for j in range(c * SCALE_CHUNKS, (c + 1) * SCALE_CHUNKS):
                 load_words(j, 1)
 
@@ -121,13 +126,7 @@ def tile_multiheadlatentattention_pb_kernel(tc, x, freq_cis, Wq_words, Wq_scales
         x_codes = keep.tile([P, TOKEN_TILES, GROUPS, P], U32, align_bytes=64)
         x_scales = keep.tile([P, TOKEN_TILES, GROUPS, P], U8, align_bytes=64)
 
-        turned = turned_pool.tile([P, 2, 2, P], F32)
-        for i in range(WARM_FIRST):
-            nc.tensor.matmul(
-                out=turned[:].rearrange("p g u r -> p (g u r)"), lhsT=zeros[:, :P], rhs=zeros[:], start=True, stop=True
-            )
-
-        def turn(m):
+        def turn(m, turned_pool):
             x_words = x_tiles[m][:].bitcast(F32)
             grouped = x_in.tile([P, GROUPS, P, PACK], BF16, align_bytes=64)
             grouped_words = grouped[:].bitcast(F32)
@@ -152,8 +151,8 @@ def tile_multiheadlatentattention_pb_kernel(tc, x, freq_cis, Wq_words, Wq_scales
                 )
 
         def passes(target, j, m, first_col, width):
-            plane = w_planes[j // SCALE_CHUNKS]
-            plane_col = (j % SCALE_CHUNKS) * N_TILE + first_col
+            plane, plane_col = w_planes[j]
+            plane_col = plane_col + first_col
             for g in range(GROUPS):
                 nc.tensor.matmul_mx(
                     out=target,
@@ -189,43 +188,37 @@ def tile_multiheadlatentattention_pb_kernel(tc, x, freq_cis, Wq_words, Wq_scales
                 out=rotated, in0=rotated, in1=crossed[:].rearrange("p h e i -> p h i e"), op=ADD
             )
 
-        def multiply(j, m):
-            sums = sums_pool.tile([P, BANK_HEADS, QK], F32)
+        def multiply(pool, j, m):
+            last = (j, m) == (CHUNKS - 1, TOKEN_TILES - 1)
+            sums = pool.tile([P, BANK_HEADS, QK], F32)
             passes(sums[:].rearrange("p h d -> p (h d)"), j, m, 0, N_TILE)
             result = results.tile([P, BANK_HEADS, QK], F32)
-            rotate(sums[:, :, NOPE:], result[:, :, NOPE:], m, nc.gpsimd)
+            rotate(sums[:, :, NOPE:], result[:, :, NOPE:], m, nc.vector if last else nc.gpsimd)
             nc.scalar.copy(out=result[:, :, :NOPE], in_=sums[:, :, :NOPE])
             nc.sync.dma_start(
                 out=out_rows_dram[m * P : (m + 1) * P, j * N_TILE : (j + 1) * N_TILE],
                 in_=result[:].rearrange("p h d -> p (h d)"),
             )
 
-        def multiply_last(j, m):
-            result = results.tile([P, BANK_HEADS, QK], F32)
-            rows = slice(m * P, (m + 1) * P)
-            heads = slice(j * BANK_HEADS, (j + 1) * BANK_HEADS)
-            sums = sums_pool.tile([P, BANK_HEADS, ROPE], F32)
-            for h in range(BANK_HEADS):
-                passes(sums[:, h, :], j, m, h * QK + NOPE, ROPE)
-            rotate(sums[:], result[:, :, NOPE:], m, nc.vector)
-            nc.sync.dma_start(out=out_heads_dram[rows, heads, NOPE:], in_=result[:, :, NOPE:])
-            sums = sums_pool.tile([P, BANK_HEADS, NOPE], F32)
-            for h in range(BANK_HEADS):
-                passes(sums[:, h, :], j, m, h * QK, NOPE)
-            nc.scalar.copy(out=result[:, :, :NOPE], in_=sums[:])
-            nc.sync.dma_start(out=out_heads_dram[rows, heads, :NOPE], in_=result[:, :, :NOPE])
-
-        turn(0)
-        turn(1)
-        multiply(0, 0)
-        multiply(0, 1)
-        turn(2)
-        turn(3)
-        multiply(0, 2)
-        multiply(0, 3)
-        for j in range(1, CHUNKS):
-            for m in range(TOKEN_TILES):
-                if (j, m) == (CHUNKS - 1, TOKEN_TILES - 1):
-                    multiply_last(j, m)
-                else:
-                    multiply(j, m)
+        with tc.psum_pool(name="turned", bufs=4) as turned_pool:
+            turned = turned_pool.tile([P, 2, 2, P], F32)
+            for i in range(WARM_FIRST):
+                nc.tensor.matmul(
+                    out=turned[:].rearrange("p g u r -> p (g u r)"),
+                    lhsT=zeros[:, :P],
+                    rhs=zeros[:],
+                    start=True,
+                    stop=True,
+                )
+            turn(0, turned_pool)
+            turn(1, turned_pool)
+            multiply(sums_pool, 0, 0)
+            multiply(sums_pool, 0, 1)
+            turn(2, turned_pool)
+            turn(3, turned_pool)
+        with tc.psum_pool(name="sums_b", bufs=4, reuse_waits="tile") as sums_b:
+            pools = (sums_pool, sums_b)
+            for j in range(CHUNKS):
+                for m in range(TOKEN_TILES):
+                    if j > 0 or m > 1:
+                        multiply(pools[m % 2], j, m)

@@ -37,6 +37,7 @@ SCALE_CHUNKS = 2
 SCALE_COLS = SCALE_CHUNKS * N_TILE
 
 WARM_FIRST = 4
+WARM_BETWEEN = 2
 
 PLANE_RUNS = ((0, 1), (1, 1), (2, 2), (4, 2), (6, 2))
 
@@ -201,20 +202,26 @@ def tile_multiheadlatentattention_pb_kernel(tc, x, freq_cis, Wq_words, Wq_scales
             )
 
         with tc.psum_pool(name="turned", bufs=4) as turned_pool:
-            turned = turned_pool.tile([P, 2, 2, P], F32)
-            for i in range(WARM_FIRST):
-                nc.tensor.matmul(
-                    out=turned[:].rearrange("p g u r -> p (g u r)"),
-                    lhsT=zeros[:, :P],
-                    rhs=zeros[:],
-                    start=True,
-                    stop=True,
-                )
+
+            def dummies(count):
+                turned = turned_pool.tile([P, 2, 2, P], F32)
+                for i in range(count):
+                    nc.tensor.matmul(
+                        out=turned[:].rearrange("p g u r -> p (g u r)"),
+                        lhsT=zeros[:, :P],
+                        rhs=zeros[:],
+                        start=True,
+                        stop=True,
+                    )
+
+            dummies(WARM_FIRST)
             turn(0, turned_pool)
+            dummies(WARM_BETWEEN)
             turn(1, turned_pool)
             multiply(sums_pool, 0, 0)
             multiply(sums_pool, 0, 1)
             turn(2, turned_pool)
+            dummies(WARM_BETWEEN)
             turn(3, turned_pool)
         with tc.psum_pool(name="sums_b", bufs=4, reuse_waits="tile") as sums_b:
             pools = (sums_pool, sums_b)

@@ -38,8 +38,16 @@ SCALE_COLS = SCALE_CHUNKS * N_TILE
 
 WARM_FIRST = 4
 WARM_BETWEEN = 2
+SORTED_TILES = (2, 3)
 
 PLANE_RUNS = ((0, 1), (1, 1), (2, 2), (4, 2), (6, 2))
+
+SPLIT_HEADS = 2 * BANK_HEADS
+PLAIN_CHUNKS = CHUNKS - 2
+ROTATED_CHUNK = PLAIN_CHUNKS
+KEPT_CHUNK = PLAIN_CHUNKS + 1
+PLAIN_BEHIND_ROTATED = 2
+GPSIMD_ADDS = 2
 
 FLOPS = 2 * TOKENS * K * N
 
@@ -55,12 +63,14 @@ def tile_multiheadlatentattention_pb_kernel(tc, x, freq_cis, Wq_words, Wq_scales
     with tc.tile_pool(name="keep", bufs=1) as keep, tc.tile_pool(
         name="x_in", bufs=TOKEN_TILES
     ) as x_in, tc.tile_pool(name="w_in", bufs=CHUNKS) as w_in, tc.tile_pool(
-        name="s_in", bufs=len(PLANE_RUNS)
+        name="s_in", bufs=len(PLANE_RUNS) + 2
     ) as s_in, tc.tile_pool(name="results", bufs=32) as results, tc.tile_pool(
         name="crossed", bufs=8
     ) as crossed_pool, tc.psum_pool(
         name="sums", bufs=4, reuse_waits="tile"
-    ) as sums_pool, tc.manual_schedule(engines={mybir.EngineType.PE}):
+    ) as sums_pool, tc.manual_schedule(
+        engines={mybir.EngineType.PE, mybir.EngineType.DVE, mybir.EngineType.SP}
+    ):
         zeros = keep.tile([P, N_TILE], BF16)
         nc.vector.memset(zeros[:], 0.0)
         w_planes = {}
@@ -101,6 +111,29 @@ def tile_multiheadlatentattention_pb_kernel(tc, x, freq_cis, Wq_words, Wq_scales
                 )
             w_chunks.append(w_chunk)
 
+        def load_split_words(part):
+            w_chunk = w_in.tile([P, GROUPS, 2 * N_TILE], U8, align_bytes=64)
+            for g in range(GROUPS):
+                nc.sync.dma_start(
+                    out=w_chunk[:, g, :].bitcast(I32).rearrange("p (h w) -> p h w", h=SPLIT_HEADS),
+                    in_=words_dram[:, g, PLAIN_CHUNKS * 2 * N_TILE :]
+                    .bitcast(I32)
+                    .rearrange("p (h s w) -> p h s w", h=SPLIT_HEADS, s=2)[:, :, part, :],
+                )
+            return w_chunk
+
+        def regroup_scales():
+            natural = w_planes[PLAIN_CHUNKS][0][:].bitcast(I32).rearrange(
+                "p g (h s w) -> p g h s w", h=SPLIT_HEADS, s=2
+            )
+            for j, part in ((ROTATED_CHUNK, 1), (KEPT_CHUNK, 0)):
+                plane = s_in.tile([P, GROUPS, N_TILE], U8, align_bytes=64)
+                nc.vector.tensor_copy(
+                    out=plane[:].bitcast(I32).rearrange("p g (h w) -> p g h w", h=SPLIT_HEADS),
+                    in_=natural[:, :, :, part, :],
+                )
+                w_planes[j] = (plane, 0)
+
         load_x(0)
         load_scales(0, 1)
         load_x(1)
@@ -109,10 +142,17 @@ def tile_multiheadlatentattention_pb_kernel(tc, x, freq_cis, Wq_words, Wq_scales
         load_x(3)
         load_scales(1, 1)
         load_words(1, 1)
-        for c in range(1, CHUNKS // SCALE_CHUNKS):
+        split_words = {}
+        for c in (1, 3, 2):
             load_scales(c * SCALE_CHUNKS, SCALE_CHUNKS)
-            for j in range(c * SCALE_CHUNKS, (c + 1) * SCALE_CHUNKS):
-                load_words(j, 1)
+            if c * SCALE_CHUNKS < PLAIN_CHUNKS:
+                for j in range(c * SCALE_CHUNKS, (c + 1) * SCALE_CHUNKS):
+                    load_words(j, 1)
+            else:
+                split_words[ROTATED_CHUNK] = load_split_words(1)
+        split_words[KEPT_CHUNK] = load_split_words(0)
+        w_chunks.append(split_words[ROTATED_CHUNK])
+        w_chunks.append(split_words[KEPT_CHUNK])
 
         cos_pair = keep.tile([P, TOKEN_TILES, PAIRS, 2], F32)
         sin_signed = keep.tile([P, TOKEN_TILES, 2, PAIRS], F32)
@@ -127,6 +167,18 @@ def tile_multiheadlatentattention_pb_kernel(tc, x, freq_cis, Wq_words, Wq_scales
         x_codes = keep.tile([P, TOKEN_TILES, GROUPS, P], U32, align_bytes=64)
         x_scales = keep.tile([P, TOKEN_TILES, GROUPS, P], U8, align_bytes=64)
 
+        sorted_tiles = {}
+
+        def sort_words(m):
+            x_sorted = x_in.tile([P, GROUPS, 2, P], F32)
+            x_words = x_tiles[m][:].bitcast(F32).rearrange("r (g p u) -> r g u p", g=GROUPS, u=2)
+            for half in range(2):
+                nc.vector.tensor_copy(
+                    out=x_sorted[:, 2 * half : 2 * half + 2, :, :],
+                    in_=x_words[:, 2 * half : 2 * half + 2, :, :],
+                )
+            sorted_tiles[m] = x_sorted
+
         def turn(m, turned_pool):
             x_words = x_tiles[m][:].bitcast(F32)
             grouped = x_in.tile([P, GROUPS, P, PACK], BF16, align_bytes=64)
@@ -136,11 +188,11 @@ def tile_multiheadlatentattention_pb_kernel(tc, x, freq_cis, Wq_words, Wq_scales
                 for gg in range(2):
                     g = 2 * half + gg
                     for u in range(2):
-                        nc.tensor.transpose(
-                            out=turned[:, gg, u, :],
-                            in_=x_words[:, g * WORDS_PER_GROUP + u : (g + 1) * WORDS_PER_GROUP : 2],
-                            identity=identity[:],
-                        )
+                        if m in sorted_tiles:
+                            words = sorted_tiles[m][:, g, u, :]
+                        else:
+                            words = x_words[:, g * WORDS_PER_GROUP + u : (g + 1) * WORDS_PER_GROUP : 2]
+                        nc.tensor.transpose(out=turned[:, gg, u, :], in_=words, identity=identity[:])
                 nc.scalar.copy(
                     out=grouped_words[:, 2 * half : 2 * half + 2, :, :],
                     in_=turned[:].rearrange("p g u r -> p g r u"),
@@ -165,8 +217,8 @@ def tile_multiheadlatentattention_pb_kernel(tc, x, freq_cis, Wq_words, Wq_scales
                     stop=(g == GROUPS - 1),
                 )
 
-        def rotate(rope_sums, rope_result, m, adder):
-            crossed = crossed_pool.tile([P, BANK_HEADS, 2, PAIRS], F32)
+        def rotate_products(rope_sums, rope_result, m, heads):
+            crossed = crossed_pool.tile([P, heads, 2, PAIRS], F32)
             pairs = rope_sums.rearrange("p h (i e) -> p h i e", e=2)
             nc.vector.tensor_tensor(
                 out=rope_result,
@@ -174,27 +226,33 @@ def tile_multiheadlatentattention_pb_kernel(tc, x, freq_cis, Wq_words, Wq_scales
                 in1=cos_pair[:, m, :, :]
                 .rearrange("p i e -> p (i e)")
                 .unsqueeze(1)
-                .to_broadcast([P, BANK_HEADS, ROPE]),
+                .to_broadcast([P, heads, ROPE]),
                 op=MULT,
             )
             for e in range(2):
                 nc.vector.tensor_tensor(
                     out=crossed[:, :, e, :],
                     in0=pairs[:, :, :, 1 - e],
-                    in1=sin_signed[:, m, e, :].unsqueeze(1).to_broadcast([P, BANK_HEADS, PAIRS]),
+                    in1=sin_signed[:, m, e, :].unsqueeze(1).to_broadcast([P, heads, PAIRS]),
                     op=MULT,
                 )
+            return crossed
+
+        def rotate_add(rope_result, crossed, adder):
             rotated = rope_result.rearrange("p h (i e) -> p h i e", e=2)
             adder.tensor_tensor(
                 out=rotated, in0=rotated, in1=crossed[:].rearrange("p h e i -> p h i e"), op=ADD
             )
 
-        def multiply(pool, j, m):
-            last = (j, m) == (CHUNKS - 1, TOKEN_TILES - 1)
+        def product(pool, j, m):
             sums = pool.tile([P, BANK_HEADS, QK], F32)
             passes(sums[:].rearrange("p h d -> p (h d)"), j, m, 0, N_TILE)
+            return sums
+
+        def finish(sums, j, m):
             result = results.tile([P, BANK_HEADS, QK], F32)
-            rotate(sums[:, :, NOPE:], result[:, :, NOPE:], m, nc.vector if last else nc.gpsimd)
+            crossed = rotate_products(sums[:, :, NOPE:], result[:, :, NOPE:], m, BANK_HEADS)
+            rotate_add(result[:, :, NOPE:], crossed, nc.gpsimd)
             nc.scalar.copy(out=result[:, :, :NOPE], in_=sums[:, :, :NOPE])
             nc.sync.dma_start(
                 out=out_rows_dram[m * P : (m + 1) * P, j * N_TILE : (j + 1) * N_TILE],
@@ -218,14 +276,55 @@ def tile_multiheadlatentattention_pb_kernel(tc, x, freq_cis, Wq_words, Wq_scales
             turn(0, turned_pool)
             dummies(WARM_BETWEEN)
             turn(1, turned_pool)
-            multiply(sums_pool, 0, 0)
-            multiply(sums_pool, 0, 1)
-            turn(2, turned_pool)
+            for m in SORTED_TILES:
+                sort_words(m)
+            first_banks = [product(sums_pool, 0, m) for m in range(2)]
+            turn(SORTED_TILES[0], turned_pool)
             dummies(WARM_BETWEEN)
-            turn(3, turned_pool)
+            turn(SORTED_TILES[1], turned_pool)
+            for m in range(2):
+                finish(first_banks[m], 0, m)
         with tc.psum_pool(name="sums_b", bufs=4, reuse_waits="tile") as sums_b:
             pools = (sums_pool, sums_b)
-            for j in range(CHUNKS):
+
+            def split_product(j, m):
+                sums = pools[m % 2].tile([P, SPLIT_HEADS, ROPE], F32)
+                passes(sums[:].rearrange("p h d -> p (h d)"), j, m, 0, N_TILE)
+                return sums
+
+            def store_split(result, m, first_feature):
+                nc.sync.dma_start(
+                    out=out_heads_dram[
+                        m * P : (m + 1) * P, HEADS - SPLIT_HEADS :, first_feature : first_feature + ROPE
+                    ],
+                    in_=result[:],
+                )
+
+            def rotated_chunk():
+                waiting = []
+                for m in range(TOKEN_TILES):
+                    sums = split_product(ROTATED_CHUNK, m)
+                    result = results.tile([P, SPLIT_HEADS, ROPE], F32)
+                    crossed = rotate_products(sums[:], result[:], m, SPLIT_HEADS)
+                    if m < GPSIMD_ADDS:
+                        rotate_add(result[:], crossed, nc.gpsimd)
+                        store_split(result, m, NOPE)
+                    else:
+                        waiting.append((result, crossed, m))
+                for result, crossed, m in waiting:
+                    rotate_add(result[:], crossed, nc.vector)
+                    store_split(result, m, NOPE)
+
+            for j in range(PLAIN_CHUNKS):
+                if j == PLAIN_CHUNKS - PLAIN_BEHIND_ROTATED - 1:
+                    regroup_scales()
+                if j == PLAIN_CHUNKS - PLAIN_BEHIND_ROTATED:
+                    rotated_chunk()
                 for m in range(TOKEN_TILES):
                     if j > 0 or m > 1:
-                        multiply(pools[m % 2], j, m)
+                        finish(product(pools[m % 2], j, m), j, m)
+            for m in range(TOKEN_TILES):
+                sums = split_product(KEPT_CHUNK, m)
+                result = results.tile([P, SPLIT_HEADS, NOPE], F32)
+                nc.scalar.copy(out=result[:], in_=sums[:])
+                store_split(result, m, 0)

import concourse.bass as bass
import concourse.mybir as mybir
import concourse.tile as tile
from concourse.masks import make_identity

F32 = mybir.dt.float32
BF16 = mybir.dt.bfloat16
I32 = mybir.dt.int32
U32 = mybir.dt.uint32
U8 = mybir.dt.uint8
FP8X4 = mybir.dt.float8_e4m3fn_x4
FP4X4 = mybir.dt.float4_e2m1fn_x4
MULT = mybir.AluOpType.mult
ADD = mybir.AluOpType.add

P = 128
PACK = 4
K_PASS = P * PACK

TOKENS = 512
K = 2048
HEADS = 16
NOPE = 128
ROPE = 128
QK = NOPE + ROPE
PAIRS = ROPE // 2
N = HEADS * QK

TOKEN_TILES = TOKENS // P
GROUPS = K // K_PASS
N_TILE = 512
BANK_HEADS = N_TILE // QK
CHUNKS = N // N_TILE
WORDS_PER_GROUP = K_PASS // 2

SCALE_CHUNKS = 2
SCALE_COLS = SCALE_CHUNKS * N_TILE

WARM_FIRST = 4
WARM_BETWEEN = 2
SORTED_TILES = (2, 3)

PLANE_RUNS = ((0, 1), (1, 1), (2, 2), (4, 2), (6, 2))

SPLIT_HEADS = 2 * BANK_HEADS
PLAIN_CHUNKS = CHUNKS - 2
ROTATED_CHUNK = PLAIN_CHUNKS
KEPT_CHUNK = PLAIN_CHUNKS + 1
PLAIN_BEHIND_ROTATED = 2
GPSIMD_ADDS = 2

FLOPS = 2 * TOKENS * K * N


def tile_multiheadlatentattention_pb_kernel(tc, x, freq_cis, Wq_words, Wq_scales, out):
    nc = tc.nc
    x_rows_dram = x.rearrange("b t k -> (b t) k")
    out_rows_dram = out.rearrange("b t h d -> (b t) (h d)")
    out_heads_dram = out.rearrange("b t h d -> (b t) h d")
    words_dram = Wq_words.rearrange("g p b -> p g b")
    scales_dram = Wq_scales.rearrange("g q n -> q g n")

    with tc.tile_pool(name="keep", bufs=1) as keep, tc.tile_pool(
        name="x_in", bufs=TOKEN_TILES
    ) as x_in, tc.tile_pool(name="w_in", bufs=CHUNKS) as w_in, tc.tile_pool(
        name="s_in", bufs=len(PLANE_RUNS) + 2
    ) as s_in, tc.tile_pool(name="results", bufs=32) as results, tc.tile_pool(
        name="crossed", bufs=8
    ) as crossed_pool, tc.psum_pool(
        name="sums", bufs=4, reuse_waits="tile"
    ) as sums_pool, tc.manual_schedule(
        engines={mybir.EngineType.PE, mybir.EngineType.DVE, mybir.EngineType.SP}
    ):
        zeros = keep.tile([P, N_TILE], BF16)
        nc.vector.memset(zeros[:], 0.0)
        w_planes = {}
        for first, count in PLANE_RUNS:
            plane = s_in.tile([P, GROUPS, count * N_TILE], U8, align_bytes=64)
            nc.vector.memset(plane[:].bitcast(I32), 0)
            for j in range(first, first + count):
                w_planes[j] = (plane, (j - first) * N_TILE)

        table = keep.tile([P, TOKEN_TILES, PAIRS, 2], BF16)
        nc.scalar.dma_start(out=table[:], in_=freq_cis.rearrange("(m p) i e -> p m i e", p=P))
        primed = keep.tile([P, 1], BF16)
        nc.scalar.copy(out=primed[:], in_=zeros[:, 0:1])

        def load_scales(j, count):
            for r in range(4):
                nc.sync.dma_start(
                    out=w_planes[j][0][r : P : 32, :, :].bitcast(I32),
                    in_=scales_dram[r : 16 : 4, :, j * N_TILE : (j + count) * N_TILE].bitcast(I32),
                )

        x_tiles = []

        def load_x(m):
            x_rows = x_in.tile([P, K], BF16)
            nc.sync.dma_start(out=x_rows[:], in_=x_rows_dram[m * P : (m + 1) * P, :])
            x_tiles.append(x_rows)

        w_chunks = []

        def load_words(j, pieces):
            w_chunk = w_in.tile([P, GROUPS, 2 * N_TILE], U8, align_bytes=64)
            step = GROUPS // pieces
            for g0 in range(0, GROUPS, step):
                nc.sync.dma_start(
                    out=w_chunk[:, g0 : g0 + step, :].bitcast(I32),
                    in_=words_dram[:, g0 : g0 + step, j * 2 * N_TILE : (j + 1) * 2 * N_TILE].bitcast(I32),
                )
            w_chunks.append(w_chunk)

        def load_split_words(part):
            w_chunk = w_in.tile([P, GROUPS, 2 * N_TILE], U8, align_bytes=64)
            for g in range(GROUPS):
                nc.sync.dma_start(
                    out=w_chunk[:, g, :].bitcast(I32).rearrange("p (h w) -> p h w", h=SPLIT_HEADS),
                    in_=words_dram[:, g, PLAIN_CHUNKS * 2 * N_TILE :]
                    .bitcast(I32)
                    .rearrange("p (h s w) -> p h s w", h=SPLIT_HEADS, s=2)[:, :, part, :],
                )
            return w_chunk

        def regroup_scales():
            natural = w_planes[PLAIN_CHUNKS][0][:].bitcast(I32).rearrange(
                "p g (h s w) -> p g h s w", h=SPLIT_HEADS, s=2
            )
            for j, part in ((ROTATED_CHUNK, 1), (KEPT_CHUNK, 0)):
                plane = s_in.tile([P, GROUPS, N_TILE], U8, align_bytes=64)
                nc.vector.tensor_copy(
                    out=plane[:].bitcast(I32).rearrange("p g (h w) -> p g h w", h=SPLIT_HEADS),
                    in_=natural[:, :, :, part, :],
                )
                w_planes[j] = (plane, 0)

        load_x(0)
        load_scales(0, 1)
        load_x(1)
        load_words(0, 2)
        load_x(2)
        load_x(3)
        load_scales(1, 1)
        load_words(1, 1)
        split_words = {}
        for c in (1, 3, 2):
            load_scales(c * SCALE_CHUNKS, SCALE_CHUNKS)
            if c * SCALE_CHUNKS < PLAIN_CHUNKS:
                for j in range(c * SCALE_CHUNKS, (c + 1) * SCALE_CHUNKS):
                    load_words(j, 1)
            else:
                split_words[ROTATED_CHUNK] = load_split_words(1)
        split_words[KEPT_CHUNK] = load_split_words(0)
        w_chunks.append(split_words[ROTATED_CHUNK])
        w_chunks.append(split_words[KEPT_CHUNK])

        cos_pair = keep.tile([P, TOKEN_TILES, PAIRS, 2], F32)
        sin_signed = keep.tile([P, TOKEN_TILES, 2, PAIRS], F32)
        nc.vector.tensor_copy(
            out=cos_pair[:], in_=table[:, :, :, 0:1].to_broadcast([P, TOKEN_TILES, PAIRS, 2])
        )
        nc.vector.tensor_scalar_mul(out=sin_signed[:, :, 0, :], in0=table[:, :, :, 1], scalar1=-1.0)
        nc.vector.tensor_copy(out=sin_signed[:, :, 1, :], in_=table[:, :, :, 1])

        identity = keep.tile([P, P], F32)
        make_identity(nc, identity[:])
        x_codes = keep.tile([P, TOKEN_TILES, GROUPS, P], U32, align_bytes=64)
        x_scales = keep.tile([P, TOKEN_TILES, GROUPS, P], U8, align_bytes=64)

        sorted_tiles = {}

        def sort_words(m):
            x_sorted = x_in.tile([P, GROUPS, 2, P], F32)
            x_words = x_tiles[m][:].bitcast(F32).rearrange("r (g p u) -> r g u p", g=GROUPS, u=2)
            for half in range(2):
                nc.vector.tensor_copy(
                    out=x_sorted[:, 2 * half : 2 * half + 2, :, :],
                    in_=x_words[:, 2 * half : 2 * half + 2, :, :],
                )
            sorted_tiles[m] = x_sorted

        def turn(m, turned_pool):
            x_words = x_tiles[m][:].bitcast(F32)
            grouped = x_in.tile([P, GROUPS, P, PACK], BF16, align_bytes=64)
            grouped_words = grouped[:].bitcast(F32)
            for half in range(2):
                turned = turned_pool.tile([P, 2, 2, P], F32)
                for gg in range(2):
                    g = 2 * half + gg
                    for u in range(2):
                        if m in sorted_tiles:
                            words = sorted_tiles[m][:, g, u, :]
                        else:
                            words = x_words[:, g * WORDS_PER_GROUP + u : (g + 1) * WORDS_PER_GROUP : 2]
                        nc.tensor.transpose(out=turned[:, gg, u, :], in_=words, identity=identity[:])
                nc.scalar.copy(
                    out=grouped_words[:, 2 * half : 2 * half + 2, :, :],
                    in_=turned[:].rearrange("p g u r -> p g r u"),
                )
                nc.vector.quantize_mx(
                    out=x_codes[:, m, 2 * half : 2 * half + 2, :].rearrange("p g r -> p (g r)").bitcast(FP8X4),
                    scales=x_scales[:, m, 2 * half : 2 * half + 2, :].rearrange("p g r -> p (g r)"),
                    in_=grouped[:, 2 * half : 2 * half + 2, :, :].rearrange("p g r t -> p (g r t)"),
                )

        def passes(target, j, m, first_col, width):
            plane, plane_col = w_planes[j]
            plane_col = plane_col + first_col
            for g in range(GROUPS):
                nc.tensor.matmul_mx(
                    out=target,
                    lhsT=x_codes[:, m, g, :].bitcast(FP8X4),
                    lhsT_scale=x_scales[:, m, g, :],
                    rhs=w_chunks[j][:, g, 2 * first_col : 2 * (first_col + width)].bitcast(FP4X4),
                    rhs_scale=plane[:, g, plane_col : plane_col + width],
                    start=(g == 0),
                    stop=(g == GROUPS - 1),
                )

        def rotate_products(rope_sums, rope_result, m, heads):
            crossed = crossed_pool.tile([P, heads, 2, PAIRS], F32)
            pairs = rope_sums.rearrange("p h (i e) -> p h i e", e=2)
            nc.vector.tensor_tensor(
                out=rope_result,
                in0=rope_sums,
                in1=cos_pair[:, m, :, :]
                .rearrange("p i e -> p (i e)")
                .unsqueeze(1)
                .to_broadcast([P, heads, ROPE]),
                op=MULT,
            )
            for e in range(2):
                nc.vector.tensor_tensor(
                    out=crossed[:, :, e, :],
                    in0=pairs[:, :, :, 1 - e],
                    in1=sin_signed[:, m, e, :].unsqueeze(1).to_broadcast([P, heads, PAIRS]),
                    op=MULT,
                )
            return crossed

        def rotate_add(rope_result, crossed, adder):
            rotated = rope_result.rearrange("p h (i e) -> p h i e", e=2)
            adder.tensor_tensor(
                out=rotated, in0=rotated, in1=crossed[:].rearrange("p h e i -> p h i e"), op=ADD
            )

        def product(pool, j, m):
            sums = pool.tile([P, BANK_HEADS, QK], F32)
            passes(sums[:].rearrange("p h d -> p (h d)"), j, m, 0, N_TILE)
            return sums

        def finish(sums, j, m):
            result = results.tile([P, BANK_HEADS, QK], F32)
            crossed = rotate_products(sums[:, :, NOPE:], result[:, :, NOPE:], m, BANK_HEADS)
            rotate_add(result[:, :, NOPE:], crossed, nc.gpsimd)
            nc.scalar.copy(out=result[:, :, :NOPE], in_=sums[:, :, :NOPE])
            nc.sync.dma_start(
                out=out_rows_dram[m * P : (m + 1) * P, j * N_TILE : (j + 1) * N_TILE],
                in_=result[:].rearrange("p h d -> p (h d)"),
            )

        with tc.psum_pool(name="turned", bufs=4) as turned_pool:

            def dummies(count):
                turned = turned_pool.tile([P, 2, 2, P], F32)
                for i in range(count):
                    nc.tensor.matmul(
                        out=turned[:].rearrange("p g u r -> p (g u r)"),
                        lhsT=zeros[:, :P],
                        rhs=zeros[:],
                        start=True,
                        stop=True,
                    )

            dummies(WARM_FIRST)
            turn(0, turned_pool)
            dummies(WARM_BETWEEN)
            turn(1, turned_pool)
            for m in SORTED_TILES:
                sort_words(m)
            first_banks = [product(sums_pool, 0, m) for m in range(2)]
            turn(SORTED_TILES[0], turned_pool)
            dummies(WARM_BETWEEN)
            turn(SORTED_TILES[1], turned_pool)
            for m in range(2):
                finish(first_banks[m], 0, m)
        with tc.psum_pool(name="sums_b", bufs=4, reuse_waits="tile") as sums_b:
            pools = (sums_pool, sums_b)

            def split_product(j, m):
                sums = pools[m % 2].tile([P, SPLIT_HEADS, ROPE], F32)
                passes(sums[:].rearrange("p h d -> p (h d)"), j, m, 0, N_TILE)
                return sums

            def store_split(result, m, first_feature):
                nc.sync.dma_start(
                    out=out_heads_dram[
                        m * P : (m + 1) * P, HEADS - SPLIT_HEADS :, first_feature : first_feature + ROPE
                    ],
                    in_=result[:],
                )

            def rotated_chunk():
                waiting = []
                for m in range(TOKEN_TILES):
                    sums = split_product(ROTATED_CHUNK, m)
                    result = results.tile([P, SPLIT_HEADS, ROPE], F32)
                    crossed = rotate_products(sums[:], result[:], m, SPLIT_HEADS)
                    if m < GPSIMD_ADDS:
                        rotate_add(result[:], crossed, nc.gpsimd)
                        store_split(result, m, NOPE)
                    else:
                        waiting.append((result, crossed, m))
                for result, crossed, m in waiting:
                    rotate_add(result[:], crossed, nc.vector)
                    store_split(result, m, NOPE)

            for j in range(PLAIN_CHUNKS):
                if j == PLAIN_CHUNKS - PLAIN_BEHIND_ROTATED - 1:
                    regroup_scales()
                if j == PLAIN_CHUNKS - PLAIN_BEHIND_ROTATED:
                    rotated_chunk()
                for m in range(TOKEN_TILES):
                    if j > 0 or m > 1:
                        finish(product(pools[m % 2], j, m), j, m)
            for m in range(TOKEN_TILES):
                sums = split_product(KEPT_CHUNK, m)
                result = results.tile([P, SPLIT_HEADS, NOPE], F32)
                nc.scalar.copy(out=result[:], in_=sums[:])
                store_split(result, m, 0)
